import numpy as np
import ml_dtypes


def mxq(x, axis, fmt="e4m3"):
    dtype, down = {"e4m3": (ml_dtypes.float8_e4m3fn, 7), "e5m2": (ml_dtypes.float8_e5m2, 14)}[fmt]
    v = np.moveaxis(np.asarray(x, np.float32).astype(ml_dtypes.bfloat16).astype(np.float64), axis, -1)
    blocks = v.reshape(v.shape[:-1] + (-1, 32))
    amax = np.abs(blocks).max(-1, keepdims=True)
    byte = np.maximum(np.where(amax > 0, np.frexp(amax)[1] - 1 + 127, 0) - down, 1)
    scale = np.exp2(byte - 127.0)
    codes = (blocks / scale).astype(np.float32).astype(dtype).astype(np.float64)
    return np.moveaxis((codes * scale).reshape(v.shape), -1, axis)


WIDE = False


def mx_kscale(k):
    if not WIDE:
        return np.ones(k)
    levels = np.array([10, -10, 5, -5, 0])
    if k % 512:
        return np.exp2(np.random.permutation(np.resize(levels, k // 32))).repeat(32)
    a = np.empty((k // 512, 16))
    for p in range(k // 512):
        a[p, :8] = np.random.permutation(np.resize(levels, 8))
        for g in range(8):
            far = levels[np.abs(levels - a[p, g]) >= 10]
            a[p, g + 8] = far[np.random.randint(len(far))]
    return np.exp2(a.ravel()).repeat(32)


BF16 = ml_dtypes.bfloat16


def bf(x):
    return np.asarray(x, np.float32).astype(BF16)


def f64(x):
    return np.asarray(x).astype(np.float64)


L, B, D, F, TC = 8, 4096, 512, 1024, 4
EPS = 1e-5
NT = 100
ERF_C = 1.0 / np.cumprod(2.0 * np.arange(NT) + 1.0)


def erf(v):
    a = np.minimum(np.abs(v), 6.0)
    q = 2.0 * a * a
    acc = np.full_like(q, ERF_C[-1])
    for c in ERF_C[-2::-1]:
        acc = acc * q + c
    return np.sign(v) * (2.0 / np.sqrt(np.pi)) * a * np.exp(-a * a) * acc


def gelu(v):
    return 0.5 * v * (1.0 + erf(v / np.sqrt(2.0)))


def layer_norm(x, g, b):
    m = x.mean(-1, keepdims=True)
    v = ((x - m) ** 2).mean(-1, keepdims=True)
    return (x - m) / np.sqrt(v + EPS) * g + b


def setup_inputs():
    s, t = mx_kscale(D), mx_kscale(F)
    return {"z": bf(np.random.standard_normal((B, D)) * s),
            "W1": bf(np.random.standard_normal((D, F)) / np.sqrt(D) / s[:, None]),
            "b1": bf(np.random.standard_normal(F) * 0.3),
            "g1": bf((1.0 + 0.1 * np.random.standard_normal(F)) * t),
            "be1": bf(0.1 * np.random.standard_normal(F) * t),
            "W2": bf(np.random.standard_normal((F, D)) / np.sqrt(F) / t[:, None]),
            "b2": bf(np.random.standard_normal(D) * 0.3),
            "g2": bf(1.0 + 0.1 * np.random.standard_normal(D)),
            "be2": bf(0.1 * np.random.standard_normal(D))}


def reference(z, W1, b1, g1, be1, W2, b2, g2, be2):
    h = gelu((mxq(f64(z), 1, "e4m3") @ mxq(f64(W1), 0, "e4m3")) + f64(b1))
    h = layer_norm(h, f64(g1), f64(be1))
    return layer_norm((mxq(h, 1, "e4m3") @ mxq(f64(W2), 0, "e4m3")) + f64(b2), f64(g2), f64(be2))

@@ -1,0 +1,252 @@
+from contextlib import ExitStack
+
+import concourse.mybir as mybir
+from concourse.masks import make_identity
+
+B, D, F = 4096, 512, 1024
+EPS = 1e-5
+FLOPS = 2 * B * D * F * 2
+
+F32 = mybir.dt.float32
+BF16 = mybir.dt.bfloat16
+U32 = mybir.dt.uint32
+U8 = mybir.dt.uint8
+FP8X4 = mybir.dt.float8_e4m3fn_x4
+ALU = mybir.AluOpType
+ACT = mybir.ActivationFunctionType
+
+P = 128
+NT = B // P
+GROUPS = [2,2,4,4,4,4,4,4,2,2]
+NG = len(GROUPS)
+FIRST = [sum(GROUPS[:j]) for j in range(NG)]
+BANK_DT = F32
+assert sum(GROUPS) == NT
+
+
+def tile_emaaggregator_pa_t_kernel(tc, z, W1, b1, g1, be1, W2, b2, g2, be2, out):
+    nc = tc.nc
+    z_view = z.rearrange("(p i) k -> p i k", i=NT)
+    out_view = out.rearrange("(p i) d -> p i d", i=NT)
+
+    with ExitStack() as ctx:
+        const = ctx.enter_context(tc.tile_pool(name="const", bufs=1))
+        work = ctx.enter_context(tc.tile_pool(name="work", bufs=2))
+        stats = ctx.enter_context(tc.tile_pool(name="stats", bufs=12))
+        psum = ctx.enter_context(tc.psum_pool(name="psum", bufs=2))
+
+        neg_half = const.tile([P, 1], F32, name="neg_half")
+        nc.gpsimd.memset(neg_half[:], -0.5)
+        warm = const.tile([P, 1], F32, name="warm")
+        nc.scalar.activation(out=warm[:], in_=neg_half[:], func=ACT.Gelu)
+        ident = const.tile([P, P], F32, name="ident")
+        make_identity(nc, ident[:])
+
+        zs = []
+        w1raw = []
+        w2raw = []
+
+        def load_z(grp):
+            gt = GROUPS[grp]
+            t = const.tile([P, gt, D], BF16, name="zs%d" % grp)
+            nc.sync.dma_start(out=t[:], in_=z_view[:, FIRST[grp] : FIRST[grp] + gt, :])
+            zs.append(t)
+
+        load_z(0)
+        w1_view = W1.rearrange("(p j) c -> p j c", j=4)
+        for g in range(2):
+            t = const.tile([P, 4, 512], BF16, name="w1raw%d" % g)
+            nc.sync.dma_start(out=t[:], in_=w1_view[:, :, 512 * g : 512 * (g + 1)])
+            w1raw.append(t)
+        b1n = const.tile([P, F], BF16, name="b1n")
+        nc.scalar.dma_start(out=b1n[:], in_=b1.partition_broadcast(P))
+        load_z(1)
+        for g in range(2):
+            t = const.tile([P, 4, 512], BF16, name="w2raw%d" % g)
+            nc.sync.dma_start(out=t[:], in_=W2[512 * g : 512 * (g + 1), :].rearrange("(p j) d -> p j d", j=4))
+            w2raw.append(t)
+        g1b = const.tile([P, 2, 4], BF16, name="g1b")
+        nc.scalar.dma_start(out=g1b[:], in_=g1.rearrange("(g p t) -> p g t", g=2, t=4))
+        be1b = const.tile([P, 2, 4], BF16, name="be1b")
+        nc.scalar.dma_start(out=be1b[:], in_=be1.rearrange("(g p t) -> p g t", g=2, t=4))
+        b2bc = const.tile([P, D], BF16, name="b2bc")
+        nc.scalar.dma_start(out=b2bc[:], in_=b2.partition_broadcast(P))
+        g2bc = const.tile([P, D], BF16, name="g2bc")
+        nc.scalar.dma_start(out=g2bc[:], in_=g2.partition_broadcast(P))
+        be2bc = const.tile([P, D], BF16, name="be2bc")
+        nc.scalar.dma_start(out=be2bc[:], in_=be2.partition_broadcast(P))
+        for grp in range(2, NG):
+            load_z(grp)
+
+        zq = {}
+        xhs = {}
+        hq = {}
+        w1c, w1s, w2c, w2s = [], [], [], []
+
+        def stage_z(grp):
+            gt = GROUPS[grp]
+            zg = work.tile([P, gt * P * 4], BF16, name="zg", tag="zg", align_bytes=64)
+            zgw = zg[:].bitcast(F32).rearrange("p (j r u) -> p j r u", j=gt, u=2)
+            for h in range(gt // 2):
+                zt = psum.tile([P, 2, 2, P], F32, name="zt", tag="zt", bufs=1)
+                for jj in range(2):
+                    words = zs[grp][:, 2 * h + jj, :].bitcast(F32)
+                    for u in range(2):
+                        nc.tensor.transpose(zt[:, jj, u, :], words[:, u:256:2], ident[:])
+                nc.scalar.copy(out=zgw[:, 2 * h : 2 * h + 2, :, :], in_=zt[:].rearrange("p j u r -> p j r u"))
+            zc = work.tile([P, gt * P], U32, name="zc", tag="zc", align_bytes=64)
+            zsc = work.tile([P, gt * P], U8, name="zsc", tag="zsc", align_bytes=64)
+            nc.vector.quantize_mx(out=zc[:].bitcast(FP8X4), scales=zsc[:], in_=zg[:])
+            zq[grp] = (zc, zsc)
+
+        def prep_w1():
+            for g in range(2):
+                grouped = const.tile([P, 2048], BF16, name="w1g%d" % g, align_bytes=64)
+                dst = grouped[:].rearrange("p (t m j) -> p t m j", t=4, j=4)
+                src = w1raw[g][:].rearrange("p j (m t) -> p t m j", t=4)
+                nc.vector.tensor_copy(out=dst[:, 0:2], in_=src[:, 0:2])
+                nc.scalar.copy(out=dst[:, 2:4], in_=src[:, 2:4])
+                codes = const.tile([P, 512], U32, name="w1c%d" % g, align_bytes=64)
+                scl = const.tile([P, 512], U8, name="w1s%d" % g, align_bytes=64)
+                nc.vector.quantize_mx(out=codes[:].bitcast(FP8X4), scales=scl[:], in_=grouped[:])
+                w1c.append(codes)
+                w1s.append(scl)
+
+        def prep_w2():
+            for g in range(2):
+                grouped = const.tile([P, 512, 4], BF16, name="w2g%d" % g, align_bytes=64)
+                nc.gpsimd.tensor_scalar(
+                    out=grouped[:],
+                    in0=w2raw[g][:].rearrange("p j d -> p d j"),
+                    scalar1=1.0,
+                    scalar2=0.0,
+                    op0=ALU.mult,
+                    op1=ALU.add,
+                )
+                codes = const.tile([P, 512], U32, name="w2c%d" % g, align_bytes=64)
+                scl = const.tile([P, 512], U8, name="w2s%d" % g, align_bytes=64)
+                nc.vector.quantize_mx(
+                    out=codes[:].bitcast(FP8X4), scales=scl[:], in_=grouped[:].rearrange("p d j -> p (d j)")
+                )
+                w2c.append(codes)
+                w2s.append(scl)
+
+        def stage_1(grp):
+            zc, zsc = zq[grp]
+            xhs[grp] = []
+            for i in range(GROUPS[grp]):
+                cols = slice(P * i, P * (i + 1))
+                x = work.tile([P, F], F32, name="x", tag="x", bufs=2)
+                for g in range(2):
+                    half = slice(512 * g, 512 * (g + 1))
+                    u = psum.tile([P, 512], BANK_DT, name="u", tag="u", bufs=3)
+                    nc.tensor.matmul_mx(
+                        out=u[:],
+                        lhsT=zc[:, cols].bitcast(FP8X4),
+                        lhsT_scale=zsc[:, cols],
+                        rhs=w1c[g][:].bitcast(FP8X4),
+                        rhs_scale=w1s[g][:],
+                        start=True,
+                        stop=True,
+                    )
+                    nc.vector.tensor_tensor(out=x[:, half], in0=u[:], in1=b1p[:, half], op=ALU.add)
+                a = work.tile([P, F], F32, name="a", tag="a", bufs=4)
+                sa = stats.tile([P, 1], F32, name="sa", tag="sa")
+                nc.scalar.activation(out=a[:], in_=x[:], func=ACT.Gelu, accum_out=sa[:])
+                nm = stats.tile([P, 1], F32, name="nm", tag="nm")
+                nc.gpsimd.tensor_scalar(out=nm[:], in0=sa[:], scalar1=-1.0 / F, scalar2=0.0, op0=ALU.mult, op1=ALU.add)
+                junk = work.tile([P, F], BF16, name="junk", tag="junk", bufs=1)
+                sq = stats.tile([P, 1], F32, name="sq", tag="sq")
+                nc.scalar.activation(out=junk[:], in_=a[:], func=ACT.Square, bias=nm[:], accum_out=sq[:])
+                ve = stats.tile([P, 1], F32, name="ve", tag="ve")
+                nc.gpsimd.tensor_scalar(out=ve[:], in0=sq[:], scalar1=1.0 / F, scalar2=EPS, op0=ALU.mult, op1=ALU.add)
+                rs = stats.tile([P, 1], F32, name="rs", tag="rs")
+                nc.gpsimd.tensor_tensor(out=rs[:], in0=ve[:], in1=neg_half[:], op=ALU.pow)
+                xh = work.tile([P, F], F32, name="xh", tag="xh", bufs=8)
+                nc.vector.tensor_scalar(out=xh[:], in0=a[:], scalar1=nm[:], scalar2=rs[:], op0=ALU.add, op1=ALU.mult)
+                xhs[grp].append(xh)
+
+        def stage_h(grp):
+            gt = GROUPS[grp]
+            hT = work.tile([P, 8, gt * P], BF16, name="hT", tag="hT", bufs=2)
+            hq[grp] = []
+            for g in range(2):
+                for t in range(4):
+                    blk = 4 * g + t
+                    ht = psum.tile([P, gt * P], F32, name="ht", tag="ht", bufs=2)
+                    for i in range(gt):
+                        nc.tensor.transpose(
+                            ht[:, P * i : P * (i + 1)], xhs[grp][i][:, P * blk : P * (blk + 1)], ident[:]
+                        )
+                    nc.scalar.activation(
+                        out=hT[:, blk, :],
+                        in_=ht[:],
+                        func=ACT.Identity,
+                        scale=g1c[:, blk : blk + 1],
+                        bias=be1c[:, blk : blk + 1],
+                    )
+                hg = work.tile([P, gt * P, 4], BF16, name="hg", tag="hg", bufs=4, align_bytes=64)
+                nc.vector.tensor_copy(out=hg[:], in_=hT[:, 4 * g : 4 * g + 4, :].rearrange("p t n -> p n t"))
+                hc = work.tile([P, gt * P], U32, name="hc", tag="hc", bufs=4, align_bytes=64)
+                hs = work.tile([P, gt * P], U8, name="hs", tag="hs", bufs=4, align_bytes=64)
+                nc.vector.quantize_mx(out=hc[:].bitcast(FP8X4), scales=hs[:], in_=hg[:].rearrange("p n t -> p (n t)"))
+                hq[grp].append((hc, hs))
+
+        def stage_2(grp):
+            for i in range(GROUPS[grp]):
+                cols = slice(P * i, P * (i + 1))
+                o = psum.tile([P, D], F32, name="o", tag="o", bufs=2)
+                for g in range(2):
+                    hc, hs = hq[grp][g]
+                    nc.tensor.matmul_mx(
+                        out=o[:],
+                        lhsT=hc[:, cols].bitcast(FP8X4),
+                        lhsT_scale=hs[:, cols],
+                        rhs=w2c[g][:].bitcast(FP8X4),
+                        rhs_scale=w2s[g][:],
+                        start=(g == 0),
+                        stop=(g == 1),
+                    )
+                y = work.tile([P, D], F32, name="y", tag="y", bufs=4)
+                sy = stats.tile([P, 1], F32, name="sy", tag="sy")
+                nc.vector.scalar_tensor_tensor(
+                    out=y[:], in0=o[:], scalar=1.0, in1=b2bc[:], op0=ALU.mult, op1=ALU.add, accum_out=sy[:]
+                )
+                nm2 = stats.tile([P, 1], F32, name="nm2", tag="nm2")
+                nc.gpsimd.tensor_scalar(out=nm2[:], in0=sy[:], scalar1=-1.0 / D, scalar2=0.0, op0=ALU.mult, op1=ALU.add)
+                junk2 = work.tile([P, D], BF16, name="junk2", tag="junk2", bufs=1)
+                sq2 = stats.tile([P, 1], F32, name="sq2", tag="sq2")
+                nc.scalar.activation(out=junk2[:], in_=y[:], func=ACT.Square, bias=nm2[:], accum_out=sq2[:])
+                ve2 = stats.tile([P, 1], F32, name="ve2", tag="ve2")
+                nc.gpsimd.tensor_scalar(out=ve2[:], in0=sq2[:], scalar1=1.0 / D, scalar2=EPS, op0=ALU.mult, op1=ALU.add)
+                rs2 = stats.tile([P, 1], F32, name="rs2", tag="rs2")
+                nc.gpsimd.tensor_tensor(out=rs2[:], in0=ve2[:], in1=neg_half[:], op=ALU.pow)
+                q = work.tile([P, D], F32, name="q", tag="q", bufs=2)
+                nc.vector.scalar_tensor_tensor(out=q[:], in0=y[:], scalar=nm2[:], in1=g2bc[:], op0=ALU.add, op1=ALU.mult)
+                ot = work.tile([P, D], F32, name="ot", tag="ot", bufs=4)
+                nc.vector.scalar_tensor_tensor(out=ot[:], in0=q[:], scalar=rs2[:], in1=be2bc[:], op0=ALU.mult, op1=ALU.add)
+                nc.sync.dma_start(out=out_view[:, FIRST[grp] + i, :], in_=ot[:])
+
+        stage_z(0)
+        prep_w1()
+        b1p = const.tile([P, F], BF16, name="b1p")
+        nc.vector.tensor_copy(
+            out=b1p[:].rearrange("p (g t m) -> p g t m", g=2, t=4),
+            in_=b1n[:].rearrange("p (g m t) -> p g t m", g=2, t=4),
+        )
+        g1c = const.tile([P, 8], F32, name="g1c")
+        nc.gpsimd.tensor_copy(out=g1c[:], in_=g1b[:].rearrange("p g t -> p (g t)"))
+        be1c = const.tile([P, 8], F32, name="be1c")
+        nc.gpsimd.tensor_copy(out=be1c[:], in_=be1b[:].rearrange("p g t -> p (g t)"))
+
+        for step in range(NG + 2):
+            if step >= 2:
+                stage_2(step - 2)
+            if 1 <= step <= NG:
+                stage_h(step - 1)
+            if step < NG:
+                stage_1(step)
+            if step + 1 < NG:
+                stage_z(step + 1)
+            if step == 0:
+                prep_w2()

@@ -17,11 +17,10 @@ ACT = mybir.ActivationFunctionType
 
 P = 128
 NT = B // P
-GROUPS = [2,2,4,4,4,4,4,4,2,2]
-NG = len(GROUPS)
-FIRST = [sum(GROUPS[:j]) for j in range(NG)]
+GT = 4
+NG = NT // GT
+ON_SCALAR = [3]
 BANK_DT = F32
-assert sum(GROUPS) == NT
 
 
 def tile_emaaggregator_pa_t_kernel(tc, z, W1, b1, g1, be1, W2, b2, g2, be2, out):
@@ -32,24 +31,25 @@ def tile_emaaggregator_pa_t_kernel(tc, z, W1, b1, g1, be1, W2, b2, g2, be2, out)
     with ExitStack() as ctx:
         const = ctx.enter_context(tc.tile_pool(name="const", bufs=1))
         work = ctx.enter_context(tc.tile_pool(name="work", bufs=2))
-        stats = ctx.enter_context(tc.tile_pool(name="stats", bufs=12))
+        stats = ctx.enter_context(tc.tile_pool(name="stats", bufs=3))
         psum = ctx.enter_context(tc.psum_pool(name="psum", bufs=2))
+        ctx.enter_context(tc.manual_schedule())
 
-        neg_half = const.tile([P, 1], F32, name="neg_half")
-        nc.gpsimd.memset(neg_half[:], -0.5)
-        warm = const.tile([P, 1], F32, name="warm")
-        nc.scalar.activation(out=warm[:], in_=neg_half[:], func=ACT.Gelu)
-        ident = const.tile([P, P], F32, name="ident")
-        make_identity(nc, ident[:])
+        live = {}
+
+        def ok(grp):
+            return 0 <= grp < NG
+
+        b1n = const.tile([P, F], BF16, name="b1n")
+        nc.scalar.dma_start(out=b1n[:], in_=b1.partition_broadcast(P))
 
         zs = []
         w1raw = []
         w2raw = []
 
         def load_z(grp):
-            gt = GROUPS[grp]
-            t = const.tile([P, gt, D], BF16, name="zs%d" % grp)
-            nc.sync.dma_start(out=t[:], in_=z_view[:, FIRST[grp] : FIRST[grp] + gt, :])
+            t = const.tile([P, GT, D], BF16, name="zs%d" % grp)
+            nc.sync.dma_start(out=t[:], in_=z_view[:, GT * grp : GT * (grp + 1), :])
             zs.append(t)
 
         load_z(0)
@@ -58,179 +58,328 @@ def tile_emaaggregator_pa_t_kernel(tc, z, W1, b1, g1, be1, W2, b2, g2, be2, out)
             t = const.tile([P, 4, 512], BF16, name="w1raw%d" % g)
             nc.sync.dma_start(out=t[:], in_=w1_view[:, :, 512 * g : 512 * (g + 1)])
             w1raw.append(t)
-        b1n = const.tile([P, F], BF16, name="b1n")
-        nc.scalar.dma_start(out=b1n[:], in_=b1.partition_broadcast(P))
         load_z(1)
         for g in range(2):
             t = const.tile([P, 4, 512], BF16, name="w2raw%d" % g)
             nc.sync.dma_start(out=t[:], in_=W2[512 * g : 512 * (g + 1), :].rearrange("(p j) d -> p j d", j=4))
             w2raw.append(t)
-        g1b = const.tile([P, 2, 4], BF16, name="g1b")
-        nc.scalar.dma_start(out=g1b[:], in_=g1.rearrange("(g p t) -> p g t", g=2, t=4))
-        be1b = const.tile([P, 2, 4], BF16, name="be1b")
-        nc.scalar.dma_start(out=be1b[:], in_=be1.rearrange("(g p t) -> p g t", g=2, t=4))
-        b2bc = const.tile([P, D], BF16, name="b2bc")
-        nc.scalar.dma_start(out=b2bc[:], in_=b2.partition_broadcast(P))
-        g2bc = const.tile([P, D], BF16, name="g2bc")
-        nc.scalar.dma_start(out=g2bc[:], in_=g2.partition_broadcast(P))
-        be2bc = const.tile([P, D], BF16, name="be2bc")
-        nc.scalar.dma_start(out=be2bc[:], in_=be2.partition_broadcast(P))
         for grp in range(2, NG):
             load_z(grp)
+        g1b = const.tile([P, 2, 4], BF16, name="g1b")
+        nc.sync.dma_start(out=g1b[:], in_=g1.rearrange("(g p t) -> p g t", g=2, t=4))
+        be1b = const.tile([P, 2, 4], BF16, name="be1b")
+        nc.sync.dma_start(out=be1b[:], in_=be1.rearrange("(g p t) -> p g t", g=2, t=4))
+        b2bc = const.tile([P, D], BF16, name="b2bc")
+        nc.sync.dma_start(out=b2bc[:], in_=b2.partition_broadcast(P))
+        g2bc = const.tile([P, D], BF16, name="g2bc")
+        nc.sync.dma_start(out=g2bc[:], in_=g2.partition_broadcast(P))
+        be2bc = const.tile([P, D], BF16, name="be2bc")
+        nc.sync.dma_start(out=be2bc[:], in_=be2.partition_broadcast(P))
 
-        zq = {}
-        xhs = {}
-        hq = {}
+        neg_half = const.tile([P, GT], F32, name="neg_half")
+        nc.gpsimd.memset(neg_half[:], -0.5)
+        warm = const.tile([P, 1], F32, name="warm")
+        nc.scalar.activation(out=warm[:], in_=neg_half[:, 0:1], func=ACT.Gelu)
+        ident = const.tile([P, P], F32, name="ident")
+        make_identity(nc, ident[:])
+
+        def z_transpose(grp, h):
+            if not ok(grp):
+                return
+            zt = psum.tile([P, 2, 2, P], F32, name="zt", tag="zt", bufs=1)
+            for jj in range(2):
+                words = zs[grp][:, 2 * h + jj, :].bitcast(F32)
+                for u in range(2):
+                    nc.tensor.transpose(zt[:, jj, u, :], words[:, u:256:2], ident[:])
+            live["zt", grp, h] = zt
+
+        def z_copy(grp, h):
+            if not ok(grp):
+                return
+            if h == 0:
+                live["zg", grp] = work.tile([P, GT * P * 4], BF16, name="zg", tag="zg", bufs=2, align_bytes=64)
+            zgw = live["zg", grp][:].bitcast(F32).rearrange("p (j r u) -> p j r u", j=GT, u=2)
+            nc.scalar.copy(
+                out=zgw[:, 2 * h : 2 * h + 2, :, :], in_=live["zt", grp, h][:].rearrange("p j u r -> p j r u")
+            )
+
+        def z_quantise(grp):
+            if not ok(grp):
+                return
+            zc = work.tile([P, GT * P], U32, name="zc", tag="zc", bufs=2, align_bytes=64)
+            zsc = work.tile([P, GT * P], U8, name="zsc", tag="zsc", bufs=2, align_bytes=64)
+            nc.vector.quantize_mx(out=zc[:].bitcast(FP8X4), scales=zsc[:], in_=live["zg", grp][:])
+            live["zq", grp] = (zc, zsc)
+
+        def matmul_1(grp, i):
+            if not ok(grp):
+                return
+            zc, zsc = live["zq", grp]
+            cols = slice(P * i, P * (i + 1))
+            for g in range(2):
+                u = psum.tile([P, 512], BANK_DT, name="u", tag="u", bufs=3)
+                nc.tensor.matmul_mx(
+                    out=u[:],
+                    lhsT=zc[:, cols].bitcast(FP8X4),
+                    lhsT_scale=zsc[:, cols],
+                    rhs=w1c[g][:].bitcast(FP8X4),
+                    rhs_scale=w1s[g][:],
+                    start=True,
+                    stop=True,
+                )
+                live["u", grp, i, g] = u
+
+        def add_b1(grp, i):
+            if not ok(grp):
+                return
+            x = work.tile([P, F], F32, name="x", tag="x", bufs=2)
+            for g in range(2):
+                half = slice(512 * g, 512 * (g + 1))
+                nc.vector.tensor_tensor(out=x[:, half], in0=live["u", grp, i, g][:], in1=b1p[:, half], op=ALU.add)
+            live["x", grp, i] = x
+
+        def gelu(grp, i):
+            if not ok(grp):
+                return
+            if i == 0:
+                live["sa", grp] = stats.tile([P, GT], F32, name="sa", tag="sa")
+            a = work.tile([P, F], F32, name="a", tag="a", bufs=6)
+            nc.scalar.activation(
+                out=a[:], in_=live["x", grp, i][:], func=ACT.Gelu, accum_out=live["sa", grp][:, i : i + 1]
+            )
+            live["a", grp, i] = a
+
+        def square_1(grp, i):
+            if not ok(grp):
+                return
+            if i == 0:
+                live["sq", grp] = stats.tile([P, GT], F32, name="sq", tag="sq")
+            junk = work.tile([P, F], BF16, name="junk", tag="junk", bufs=1)
+            nc.scalar.activation(
+                out=junk[:],
+                in_=live["a", grp, i][:],
+                func=ACT.Square,
+                scale=-float(F),
+                bias=live["sa", grp][:, i : i + 1],
+                accum_out=live["sq", grp][:, i : i + 1],
+            )
+
+        def neg_mean_1(grp):
+            if not ok(grp):
+                return
+            nm = stats.tile([P, GT], F32, name="nm", tag="nm")
+            nc.vector.tensor_scalar(out=nm[:], in0=live["sa", grp][:], scalar1=-1.0 / F, scalar2=None, op0=ALU.mult)
+            live["nm", grp] = nm
+
+        def var_eps_1(grp):
+            if not ok(grp):
+                return
+            ve = stats.tile([P, GT], F32, name="ve", tag="ve")
+            nc.vector.tensor_scalar(
+                out=ve[:], in0=live["sq", grp][:], scalar1=1.0 / F**3, scalar2=EPS, op0=ALU.mult, op1=ALU.add
+            )
+            live["ve", grp] = ve
+
+        def rstd_1(grp):
+            if not ok(grp):
+                return
+            rs = stats.tile([P, GT], F32, name="rs", tag="rs")
+            nc.gpsimd.tensor_tensor(out=rs[:], in0=live["ve", grp][:], in1=neg_half[:], op=ALU.pow)
+            nr = stats.tile([P, GT], F32, name="nr", tag="nr")
+            nc.gpsimd.tensor_tensor(out=nr[:], in0=live["nm", grp][:], in1=rs[:], op=ALU.mult)
+            live["rs", grp] = rs
+            live["nr", grp] = nr
+
+        def normalise(grp, i):
+            if not ok(grp):
+                return
+            col = slice(i, i + 1)
+            xh = work.tile([P, F], F32, name="xh", tag="xh", bufs=4)
+            if i in ON_SCALAR:
+                nc.scalar.activation(
+                    out=xh[:],
+                    in_=live["a", grp, i][:],
+                    func=ACT.Identity,
+                    scale=live["rs", grp][:, col],
+                    bias=live["nr", grp][:, col],
+                )
+            else:
+                nc.vector.tensor_scalar(
+                    out=xh[:],
+                    in0=live["a", grp, i][:],
+                    scalar1=live["nm", grp][:, col],
+                    scalar2=live["rs", grp][:, col],
+                    op0=ALU.add,
+                    op1=ALU.mult,
+                )
+            live["xh", grp, i] = xh
+
+        def h_transpose(grp, blk):
+            if not ok(grp):
+                return
+            ht = psum.tile([P, GT * P], F32, name="ht", tag="ht", bufs=2)
+            for i in range(GT):
+                nc.tensor.transpose(ht[:, P * i : P * (i + 1)], live["xh", grp, i][:, P * blk : P * (blk + 1)], ident[:])
+            live["ht", grp, blk] = ht
+
+        def affine_1(grp, blk):
+            if not ok(grp):
+                return
+            if blk == 0:
+                live["hT", grp] = work.tile([P, 8, GT * P], BF16, name="hT", tag="hT", bufs=2)
+            nc.scalar.activation(
+                out=live["hT", grp][:, blk, :],
+                in_=live["ht", grp, blk][:],
+                func=ACT.Identity,
+                scale=g1c[:, blk : blk + 1],
+                bias=be1c[:, blk : blk + 1],
+            )
+
+        def interleave(grp, g):
+            if not ok(grp):
+                return
+            hg = work.tile([P, GT * P, 4], BF16, name="hg", tag="hg", bufs=2, align_bytes=64)
+            nc.vector.tensor_copy(out=hg[:], in_=live["hT", grp][:, 4 * g : 4 * g + 4, :].rearrange("p t n -> p n t"))
+            live["hg", grp, g] = hg
+
+        def h_quantise(grp, g):
+            if not ok(grp):
+                return
+            hc = work.tile([P, GT * P], U32, name="hc", tag="hc", bufs=4, align_bytes=64)
+            hs = work.tile([P, GT * P], U8, name="hs", tag="hs", bufs=4, align_bytes=64)
+            nc.vector.quantize_mx(
+                out=hc[:].bitcast(FP8X4), scales=hs[:], in_=live["hg", grp, g][:].rearrange("p n t -> p (n t)")
+            )
+            live["hq", grp, g] = (hc, hs)
+
+        def matmul_2(grp, i):
+            if not ok(grp):
+                return
+            cols = slice(P * i, P * (i + 1))
+            o = psum.tile([P, D], F32, name="o", tag="o", bufs=2)
+            for g in range(2):
+                hc, hs = live["hq", grp, g]
+                nc.tensor.matmul_mx(
+                    out=o[:],
+                    lhsT=hc[:, cols].bitcast(FP8X4),
+                    lhsT_scale=hs[:, cols],
+                    rhs=w2c[g][:].bitcast(FP8X4),
+                    rhs_scale=w2s[g][:],
+                    start=(g == 0),
+                    stop=(g == 1),
+                )
+            live["o", grp, i] = o
+
+        def add_b2(grp, i):
+            if not ok(grp):
+                return
+            if i == 0:
+                live["sy", grp] = stats.tile([P, GT], F32, name="sy", tag="sy")
+            y = work.tile([P, D], F32, name="y", tag="y", bufs=4)
+            nc.vector.scalar_tensor_tensor(
+                out=y[:],
+                in0=live["o", grp, i][:],
+                scalar=1.0,
+                in1=b2bc[:],
+                op0=ALU.mult,
+                op1=ALU.add,
+                accum_out=live["sy", grp][:, i : i + 1],
+            )
+            live["y", grp, i] = y
+
+        def square_2(grp, i):
+            if not ok(grp):
+                return
+            if i == 0:
+                live["sq2", grp] = stats.tile([P, GT], F32, name="sq2", tag="sq2")
+            junk2 = work.tile([P, D], BF16, name="junk2", tag="junk2", bufs=1)
+            nc.scalar.activation(
+                out=junk2[:],
+                in_=live["y", grp, i][:],
+                func=ACT.Square,
+                scale=-float(D),
+                bias=live["sy", grp][:, i : i + 1],
+                accum_out=live["sq2", grp][:, i : i + 1],
+            )
+
+        def neg_mean_2(grp):
+            if not ok(grp):
+                return
+            nm2 = stats.tile([P, GT], F32, name="nm2", tag="nm2")
+            nc.vector.tensor_scalar(out=nm2[:], in0=live["sy", grp][:], scalar1=-1.0 / D, scalar2=None, op0=ALU.mult)
+            live["nm2", grp] = nm2
+
+        def var_eps_2(grp):
+            if not ok(grp):
+                return
+            ve2 = stats.tile([P, GT], F32, name="ve2", tag="ve2")
+            nc.vector.tensor_scalar(
+                out=ve2[:], in0=live["sq2", grp][:], scalar1=1.0 / D**3, scalar2=EPS, op0=ALU.mult, op1=ALU.add
+            )
+            live["ve2", grp] = ve2
+
+        def rstd_2(grp):
+            if not ok(grp):
+                return
+            rs2 = stats.tile([P, GT], F32, name="rs2", tag="rs2")
+            nc.gpsimd.tensor_tensor(out=rs2[:], in0=live["ve2", grp][:], in1=neg_half[:], op=ALU.pow)
+            live["rs2", grp] = rs2
+
+        def centre_gain(grp, i):
+            if not ok(grp):
+                return
+            q = work.tile([P, D], F32, name="q", tag="q", bufs=4)
+            nc.vector.scalar_tensor_tensor(
+                out=q[:],
+                in0=live["y", grp, i][:],
+                scalar=live["nm2", grp][:, i : i + 1],
+                in1=g2bc[:],
+                op0=ALU.add,
+                op1=ALU.mult,
+            )
+            live["q", grp, i] = q
+
+        def scale_shift(grp, i):
+            if not ok(grp):
+                return
+            ot = work.tile([P, D], F32, name="ot", tag="ot", bufs=4)
+            nc.vector.scalar_tensor_tensor(
+                out=ot[:],
+                in0=live["q", grp, i][:],
+                scalar=live["rs2", grp][:, i : i + 1],
+                in1=be2bc[:],
+                op0=ALU.mult,
+                op1=ALU.add,
+            )
+            live["ot", grp, i] = ot
+
+        def store(grp, i):
+            if not ok(grp):
+                return
+            nc.sync.dma_start(out=out_view[:, GT * grp + i, :], in_=live["ot", grp, i][:])
+
+        z_transpose(0, 0)
+        w1g = []
+        for g in range(2):
+            w1g.append(const.tile([P, 2048], BF16, name="w1g%d" % g, align_bytes=64))
+        dst = [w1g[g][:].rearrange("p (t m j) -> p t m j", t=4, j=4) for g in range(2)]
+        src = [w1raw[g][:].rearrange("p j (m t) -> p t m j", t=4) for g in range(2)]
         w1c, w1s, w2c, w2s = [], [], [], []
-
-        def stage_z(grp):
-            gt = GROUPS[grp]
-            zg = work.tile([P, gt * P * 4], BF16, name="zg", tag="zg", align_bytes=64)
-            zgw = zg[:].bitcast(F32).rearrange("p (j r u) -> p j r u", j=gt, u=2)
-            for h in range(gt // 2):
-                zt = psum.tile([P, 2, 2, P], F32, name="zt", tag="zt", bufs=1)
-                for jj in range(2):
-                    words = zs[grp][:, 2 * h + jj, :].bitcast(F32)
-                    for u in range(2):
-                        nc.tensor.transpose(zt[:, jj, u, :], words[:, u:256:2], ident[:])
-                nc.scalar.copy(out=zgw[:, 2 * h : 2 * h + 2, :, :], in_=zt[:].rearrange("p j u r -> p j r u"))
-            zc = work.tile([P, gt * P], U32, name="zc", tag="zc", align_bytes=64)
-            zsc = work.tile([P, gt * P], U8, name="zsc", tag="zsc", align_bytes=64)
-            nc.vector.quantize_mx(out=zc[:].bitcast(FP8X4), scales=zsc[:], in_=zg[:])
-            zq[grp] = (zc, zsc)
-
-        def prep_w1():
-            for g in range(2):
-                grouped = const.tile([P, 2048], BF16, name="w1g%d" % g, align_bytes=64)
-                dst = grouped[:].rearrange("p (t m j) -> p t m j", t=4, j=4)
-                src = w1raw[g][:].rearrange("p j (m t) -> p t m j", t=4)
-                nc.vector.tensor_copy(out=dst[:, 0:2], in_=src[:, 0:2])
-                nc.scalar.copy(out=dst[:, 2:4], in_=src[:, 2:4])
-                codes = const.tile([P, 512], U32, name="w1c%d" % g, align_bytes=64)
-                scl = const.tile([P, 512], U8, name="w1s%d" % g, align_bytes=64)
-                nc.vector.quantize_mx(out=codes[:].bitcast(FP8X4), scales=scl[:], in_=grouped[:])
-                w1c.append(codes)
-                w1s.append(scl)
-
-        def prep_w2():
-            for g in range(2):
-                grouped = const.tile([P, 512, 4], BF16, name="w2g%d" % g, align_bytes=64)
-                nc.gpsimd.tensor_scalar(
-                    out=grouped[:],
-                    in0=w2raw[g][:].rearrange("p j d -> p d j"),
-                    scalar1=1.0,
-                    scalar2=0.0,
-                    op0=ALU.mult,
-                    op1=ALU.add,
-                )
-                codes = const.tile([P, 512], U32, name="w2c%d" % g, align_bytes=64)
-                scl = const.tile([P, 512], U8, name="w2s%d" % g, align_bytes=64)
-                nc.vector.quantize_mx(
-                    out=codes[:].bitcast(FP8X4), scales=scl[:], in_=grouped[:].rearrange("p d j -> p (d j)")
-                )
-                w2c.append(codes)
-                w2s.append(scl)
-
-        def stage_1(grp):
-            zc, zsc = zq[grp]
-            xhs[grp] = []
-            for i in range(GROUPS[grp]):
-                cols = slice(P * i, P * (i + 1))
-                x = work.tile([P, F], F32, name="x", tag="x", bufs=2)
-                for g in range(2):
-                    half = slice(512 * g, 512 * (g + 1))
-                    u = psum.tile([P, 512], BANK_DT, name="u", tag="u", bufs=3)
-                    nc.tensor.matmul_mx(
-                        out=u[:],
-                        lhsT=zc[:, cols].bitcast(FP8X4),
-                        lhsT_scale=zsc[:, cols],
-                        rhs=w1c[g][:].bitcast(FP8X4),
-                        rhs_scale=w1s[g][:],
-                        start=True,
-                        stop=True,
-                    )
-                    nc.vector.tensor_tensor(out=x[:, half], in0=u[:], in1=b1p[:, half], op=ALU.add)
-                a = work.tile([P, F], F32, name="a", tag="a", bufs=4)
-                sa = stats.tile([P, 1], F32, name="sa", tag="sa")
-                nc.scalar.activation(out=a[:], in_=x[:], func=ACT.Gelu, accum_out=sa[:])
-                nm = stats.tile([P, 1], F32, name="nm", tag="nm")
-                nc.gpsimd.tensor_scalar(out=nm[:], in0=sa[:], scalar1=-1.0 / F, scalar2=0.0, op0=ALU.mult, op1=ALU.add)
-                junk = work.tile([P, F], BF16, name="junk", tag="junk", bufs=1)
-                sq = stats.tile([P, 1], F32, name="sq", tag="sq")
-                nc.scalar.activation(out=junk[:], in_=a[:], func=ACT.Square, bias=nm[:], accum_out=sq[:])
-                ve = stats.tile([P, 1], F32, name="ve", tag="ve")
-                nc.gpsimd.tensor_scalar(out=ve[:], in0=sq[:], scalar1=1.0 / F, scalar2=EPS, op0=ALU.mult, op1=ALU.add)
-                rs = stats.tile([P, 1], F32, name="rs", tag="rs")
-                nc.gpsimd.tensor_tensor(out=rs[:], in0=ve[:], in1=neg_half[:], op=ALU.pow)
-                xh = work.tile([P, F], F32, name="xh", tag="xh", bufs=8)
-                nc.vector.tensor_scalar(out=xh[:], in0=a[:], scalar1=nm[:], scalar2=rs[:], op0=ALU.add, op1=ALU.mult)
-                xhs[grp].append(xh)
-
-        def stage_h(grp):
-            gt = GROUPS[grp]
-            hT = work.tile([P, 8, gt * P], BF16, name="hT", tag="hT", bufs=2)
-            hq[grp] = []
-            for g in range(2):
-                for t in range(4):
-                    blk = 4 * g + t
-                    ht = psum.tile([P, gt * P], F32, name="ht", tag="ht", bufs=2)
-                    for i in range(gt):
-                        nc.tensor.transpose(
-                            ht[:, P * i : P * (i + 1)], xhs[grp][i][:, P * blk : P * (blk + 1)], ident[:]
-                        )
-                    nc.scalar.activation(
-                        out=hT[:, blk, :],
-                        in_=ht[:],
-                        func=ACT.Identity,
-                        scale=g1c[:, blk : blk + 1],
-                        bias=be1c[:, blk : blk + 1],
-                    )
-                hg = work.tile([P, gt * P, 4], BF16, name="hg", tag="hg", bufs=4, align_bytes=64)
-                nc.vector.tensor_copy(out=hg[:], in_=hT[:, 4 * g : 4 * g + 4, :].rearrange("p t n -> p n t"))
-                hc = work.tile([P, gt * P], U32, name="hc", tag="hc", bufs=4, align_bytes=64)
-                hs = work.tile([P, gt * P], U8, name="hs", tag="hs", bufs=4, align_bytes=64)
-                nc.vector.quantize_mx(out=hc[:].bitcast(FP8X4), scales=hs[:], in_=hg[:].rearrange("p n t -> p (n t)"))
-                hq[grp].append((hc, hs))
-
-        def stage_2(grp):
-            for i in range(GROUPS[grp]):
-                cols = slice(P * i, P * (i + 1))
-                o = psum.tile([P, D], F32, name="o", tag="o", bufs=2)
-                for g in range(2):
-                    hc, hs = hq[grp][g]
-                    nc.tensor.matmul_mx(
-                        out=o[:],
-                        lhsT=hc[:, cols].bitcast(FP8X4),
-                        lhsT_scale=hs[:, cols],
-                        rhs=w2c[g][:].bitcast(FP8X4),
-                        rhs_scale=w2s[g][:],
-                        start=(g == 0),
-                        stop=(g == 1),
-                    )
-                y = work.tile([P, D], F32, name="y", tag="y", bufs=4)
-                sy = stats.tile([P, 1], F32, name="sy", tag="sy")
-                nc.vector.scalar_tensor_tensor(
-                    out=y[:], in0=o[:], scalar=1.0, in1=b2bc[:], op0=ALU.mult, op1=ALU.add, accum_out=sy[:]
-                )
-                nm2 = stats.tile([P, 1], F32, name="nm2", tag="nm2")
-                nc.gpsimd.tensor_scalar(out=nm2[:], in0=sy[:], scalar1=-1.0 / D, scalar2=0.0, op0=ALU.mult, op1=ALU.add)
-                junk2 = work.tile([P, D], BF16, name="junk2", tag="junk2", bufs=1)
-                sq2 = stats.tile([P, 1], F32, name="sq2", tag="sq2")
-                nc.scalar.activation(out=junk2[:], in_=y[:], func=ACT.Square, bias=nm2[:], accum_out=sq2[:])
-                ve2 = stats.tile([P, 1], F32, name="ve2", tag="ve2")
-                nc.gpsimd.tensor_scalar(out=ve2[:], in0=sq2[:], scalar1=1.0 / D, scalar2=EPS, op0=ALU.mult, op1=ALU.add)
-                rs2 = stats.tile([P, 1], F32, name="rs2", tag="rs2")
-                nc.gpsimd.tensor_tensor(out=rs2[:], in0=ve2[:], in1=neg_half[:], op=ALU.pow)
-                q = work.tile([P, D], F32, name="q", tag="q", bufs=2)
-                nc.vector.scalar_tensor_tensor(out=q[:], in0=y[:], scalar=nm2[:], in1=g2bc[:], op0=ALU.add, op1=ALU.mult)
-                ot = work.tile([P, D], F32, name="ot", tag="ot", bufs=4)
-                nc.vector.scalar_tensor_tensor(out=ot[:], in0=q[:], scalar=rs2[:], in1=be2bc[:], op0=ALU.mult, op1=ALU.add)
-                nc.sync.dma_start(out=out_view[:, FIRST[grp] + i, :], in_=ot[:])
-
-        stage_z(0)
-        prep_w1()
+        for g in range(2):
+            w1c.append(const.tile([P, 512], U32, name="w1c%d" % g, align_bytes=64))
+            w1s.append(const.tile([P, 512], U8, name="w1s%d" % g, align_bytes=64))
+        nc.vector.tensor_copy(out=dst[0][:, 0:2], in_=src[0][:, 0:2])
+        nc.vector.tensor_copy(out=dst[0][:, 2:4], in_=src[0][:, 2:4])
+        nc.scalar.copy(out=dst[1][:, 2:4], in_=src[1][:, 2:4])
+        z_copy(0, 0)
+        z_transpose(0, 1)
+        z_copy(0, 1)
+        nc.vector.tensor_copy(out=dst[1][:, 0:2], in_=src[1][:, 0:2])
+        nc.vector.quantize_mx(out=w1c[0][:].bitcast(FP8X4), scales=w1s[0][:], in_=w1g[0][:])
+        z_quantise(0)
+        nc.vector.quantize_mx(out=w1c[1][:].bitcast(FP8X4), scales=w1s[1][:], in_=w1g[1][:])
         b1p = const.tile([P, F], BF16, name="b1p")
-        nc.vector.tensor_copy(
+        nc.scalar.copy(
             out=b1p[:].rearrange("p (g t m) -> p g t m", g=2, t=4),
             in_=b1n[:].rearrange("p (g m t) -> p g t m", g=2, t=4),
         )
@@ -239,14 +388,94 @@ def tile_emaaggregator_pa_t_kernel(tc, z, W1, b1, g1, be1, W2, b2, g2, be2, out)
         be1c = const.tile([P, 8], F32, name="be1c")
         nc.gpsimd.tensor_copy(out=be1c[:], in_=be1b[:].rearrange("p g t -> p (g t)"))
 
+        def prep_w2():
+            w2g = []
+            for g in range(2):
+                w2g.append(const.tile([P, 512, 4], BF16, name="w2g%d" % g, align_bytes=64))
+                nc.vector.tensor_copy(out=w2g[g][:], in_=w2raw[g][:].rearrange("p j d -> p d j"))
+            for g in range(2):
+                w2c.append(const.tile([P, 512], U32, name="w2c%d" % g, align_bytes=64))
+                w2s.append(const.tile([P, 512], U8, name="w2s%d" % g, align_bytes=64))
+                nc.vector.quantize_mx(
+                    out=w2c[g][:].bitcast(FP8X4), scales=w2s[g][:], in_=w2g[g][:].rearrange("p d j -> p (d j)")
+                )
+
         for step in range(NG + 2):
-            if step >= 2:
-                stage_2(step - 2)
-            if 1 <= step <= NG:
-                stage_h(step - 1)
-            if step < NG:
-                stage_1(step)
-            if step + 1 < NG:
-                stage_z(step + 1)
+            if True:
+                z_transpose(step + 1, 0)
+                matmul_1(step, 0)
+                matmul_1(step, 1)
+                neg_mean_1(step - 1)
+                var_eps_1(step - 1)
+                add_b1(step, 0)
+                rstd_1(step - 1)
+                normalise(step - 1, 0)
+                normalise(step - 1, 1)
+                normalise(step - 1, 3)
+                normalise(step - 1, 2)
+                h_transpose(step - 1, 0)
+                centre_gain(step - 2, 0)
+                gelu(step, 0)
+                centre_gain(step - 2, 1)
+                h_transpose(step - 1, 1)
+                var_eps_2(step - 2)
+                add_b1(step, 1)
+                rstd_2(step - 2)
+                affine_1(step - 1, 0)
+                affine_1(step - 1, 1)
+                h_transpose(step - 1, 2)
+                centre_gain(step - 2, 2)
+                z_copy(step + 1, 0)
+                h_transpose(step - 1, 3)
+                centre_gain(step - 2, 3)
+                affine_1(step - 1, 2)
+                matmul_1(step, 2)
+                scale_shift(step - 2, 0)
+                affine_1(step - 1, 3)
+                scale_shift(step - 2, 1)
+                h_transpose(step - 1, 4)
+                store(step - 2, 0)
+                gelu(step, 1)
+                interleave(step - 1, 0)
+                h_transpose(step - 1, 5)
+                store(step - 2, 1)
+                affine_1(step - 1, 4)
+                scale_shift(step - 2, 2)
+                affine_1(step - 1, 5)
+                h_transpose(step - 1, 6)
+                add_b1(step, 2)
+                store(step - 2, 2)
+                h_transpose(step - 1, 7)
+                affine_1(step - 1, 6)
+                z_transpose(step + 1, 1)
+                affine_1(step - 1, 7)
+                h_quantise(step - 1, 0)
+                matmul_1(step, 3)
+                square_1(step, 0)
+                interleave(step - 1, 1)
+                square_1(step, 1)
+                h_quantise(step - 1, 1)
+                matmul_2(step - 1, 0)
+                z_copy(step + 1, 1)
+                add_b1(step, 3)
+                gelu(step, 2)
+                matmul_2(step - 1, 1)
+                add_b2(step - 1, 0)
+                square_1(step, 2)
+                add_b2(step - 1, 1)
+                matmul_2(step - 1, 2)
+                scale_shift(step - 2, 3)
+                matmul_2(step - 1, 3)
+                gelu(step, 3)
+                z_quantise(step + 1)
+                store(step - 2, 3)
+                add_b2(step - 1, 2)
+                square_1(step, 3)
+                add_b2(step - 1, 3)
+                square_2(step - 1, 0)
+                neg_mean_2(step - 1)
+                square_2(step - 1, 1)
+                square_2(step - 1, 2)
+                square_2(step - 1, 3)
             if step == 0:
                 prep_w2()

@@ -86,7 +86,7 @@ def tile_emaaggregator_pa_t_kernel(tc, z, W1, b1, g1, be1, W2, b2, g2, be2, out)
         def z_transpose(grp, h):
             if not ok(grp):
                 return
-            zt = psum.tile([P, 2, 2, P], F32, name="zt", tag="zt", bufs=1)
+            zt = psum.tile([P, 2, 2, P], F32, name="zt", tag="bank", bufs=8)
             for jj in range(2):
                 words = zs[grp][:, 2 * h + jj, :].bitcast(F32)
                 for u in range(2):
@@ -117,7 +117,7 @@ def tile_emaaggregator_pa_t_kernel(tc, z, W1, b1, g1, be1, W2, b2, g2, be2, out)
             zc, zsc = live["zq", grp]
             cols = slice(P * i, P * (i + 1))
             for g in range(2):
-                u = psum.tile([P, 512], BANK_DT, name="u", tag="u", bufs=3)
+                u = psum.tile([P, 512], BANK_DT, name="u", tag="bank", bufs=8)
                 nc.tensor.matmul_mx(
                     out=u[:],
                     lhsT=zc[:, cols].bitcast(FP8X4),
@@ -217,7 +217,7 @@ def tile_emaaggregator_pa_t_kernel(tc, z, W1, b1, g1, be1, W2, b2, g2, be2, out)
         def h_transpose(grp, blk):
             if not ok(grp):
                 return
-            ht = psum.tile([P, GT * P], F32, name="ht", tag="ht", bufs=2)
+            ht = psum.tile([P, GT * P], F32, name="ht", tag="bank", bufs=8)
             for i in range(GT):
                 nc.tensor.transpose(ht[:, P * i : P * (i + 1)], live["xh", grp, i][:, P * blk : P * (blk + 1)], ident[:])
             live["ht", grp, blk] = ht
@@ -239,7 +239,10 @@ def tile_emaaggregator_pa_t_kernel(tc, z, W1, b1, g1, be1, W2, b2, g2, be2, out)
             if not ok(grp):
                 return
             hg = work.tile([P, GT * P, 4], BF16, name="hg", tag="hg", bufs=2, align_bytes=64)
-            nc.vector.tensor_copy(out=hg[:], in_=live["hT", grp][:, 4 * g : 4 * g + 4, :].rearrange("p t n -> p n t"))
+            nc.vector.tensor_copy(
+                out=hg[:].rearrange("p (c i) t -> p c t i", i=4),
+                in_=live["hT", grp][:, 4 * g : 4 * g + 4, :].rearrange("p t (c i) -> p c t i", i=4),
+            )
             live["hg", grp, g] = hg
 
         def h_quantise(grp, g):
@@ -256,7 +259,7 @@ def tile_emaaggregator_pa_t_kernel(tc, z, W1, b1, g1, be1, W2, b2, g2, be2, out)
             if not ok(grp):
                 return
             cols = slice(P * i, P * (i + 1))
-            o = psum.tile([P, D], F32, name="o", tag="o", bufs=2)
+            o = psum.tile([P, D], F32, name="o", tag="bank", bufs=8)
             for g in range(2):
                 hc, hs = live["hq", grp, g]
                 nc.tensor.matmul_mx(
@@ -405,76 +408,76 @@ def tile_emaaggregator_pa_t_kernel(tc, z, W1, b1, g1, be1, W2, b2, g2, be2, out)
                 z_transpose(step + 1, 0)
                 matmul_1(step, 0)
                 matmul_1(step, 1)
-                neg_mean_1(step - 1)
+                z_transpose(step + 1, 1)
+                matmul_1(step, 2)
                 var_eps_1(step - 1)
+                neg_mean_1(step - 1)
                 add_b1(step, 0)
                 rstd_1(step - 1)
                 normalise(step - 1, 0)
                 normalise(step - 1, 1)
-                normalise(step - 1, 3)
+                z_copy(step + 1, 0)
                 normalise(step - 1, 2)
+                normalise(step - 1, 3)
                 h_transpose(step - 1, 0)
                 centre_gain(step - 2, 0)
                 gelu(step, 0)
+                var_eps_2(step - 2)
                 centre_gain(step - 2, 1)
                 h_transpose(step - 1, 1)
-                var_eps_2(step - 2)
-                add_b1(step, 1)
                 rstd_2(step - 2)
-                affine_1(step - 1, 0)
-                affine_1(step - 1, 1)
+                add_b1(step, 1)
                 h_transpose(step - 1, 2)
-                centre_gain(step - 2, 2)
-                z_copy(step + 1, 0)
+                z_copy(step + 1, 1)
                 h_transpose(step - 1, 3)
-                centre_gain(step - 2, 3)
-                affine_1(step - 1, 2)
-                matmul_1(step, 2)
-                scale_shift(step - 2, 0)
-                affine_1(step - 1, 3)
-                scale_shift(step - 2, 1)
-                h_transpose(step - 1, 4)
-                store(step - 2, 0)
-                gelu(step, 1)
-                interleave(step - 1, 0)
-                h_transpose(step - 1, 5)
-                store(step - 2, 1)
-                affine_1(step - 1, 4)
-                scale_shift(step - 2, 2)
-                affine_1(step - 1, 5)
-                h_transpose(step - 1, 6)
+                affine_1(step - 1, 0)
                 add_b1(step, 2)
-                store(step - 2, 2)
+                h_transpose(step - 1, 4)
+                affine_1(step - 1, 1)
+                h_transpose(step - 1, 5)
+                h_transpose(step - 1, 6)
+                affine_1(step - 1, 2)
+                z_quantise(step + 1)
                 h_transpose(step - 1, 7)
+                affine_1(step - 1, 3)
+                centre_gain(step - 2, 2)
+                matmul_1(step, 3)
+                affine_1(step - 1, 4)
+                interleave(step - 1, 0)
+                affine_1(step - 1, 5)
                 affine_1(step - 1, 6)
-                z_transpose(step + 1, 1)
+                centre_gain(step - 2, 3)
                 affine_1(step - 1, 7)
                 h_quantise(step - 1, 0)
-                matmul_1(step, 3)
-                square_1(step, 0)
+                gelu(step, 1)
                 interleave(step - 1, 1)
-                square_1(step, 1)
+                square_1(step, 0)
                 h_quantise(step - 1, 1)
                 matmul_2(step - 1, 0)
-                z_copy(step + 1, 1)
+                square_1(step, 1)
                 add_b1(step, 3)
-                gelu(step, 2)
                 matmul_2(step - 1, 1)
-                add_b2(step - 1, 0)
-                square_1(step, 2)
-                add_b2(step - 1, 1)
+                gelu(step, 2)
+                scale_shift(step - 2, 0)
                 matmul_2(step - 1, 2)
-                scale_shift(step - 2, 3)
+                scale_shift(step - 2, 1)
+                store(step - 2, 0)
                 matmul_2(step - 1, 3)
+                square_1(step, 2)
+                scale_shift(step - 2, 2)
+                store(step - 2, 1)
+                add_b2(step - 1, 0)
+                store(step - 2, 2)
                 gelu(step, 3)
-                z_quantise(step + 1)
-                store(step - 2, 3)
+                add_b2(step - 1, 1)
                 add_b2(step - 1, 2)
                 square_1(step, 3)
                 add_b2(step - 1, 3)
+                scale_shift(step - 2, 3)
                 square_2(step - 1, 0)
                 neg_mean_2(step - 1)
                 square_2(step - 1, 1)
+                store(step - 2, 3)
                 square_2(step - 1, 2)
                 square_2(step - 1, 3)
             if step == 0:

from contextlib import ExitStack

import concourse.mybir as mybir
from concourse.masks import make_identity

B, D, F = 4096, 512, 1024
EPS = 1e-5
FLOPS = 2 * B * D * F * 2

F32 = mybir.dt.float32
BF16 = mybir.dt.bfloat16
U32 = mybir.dt.uint32
U8 = mybir.dt.uint8
FP8X4 = mybir.dt.float8_e4m3fn_x4
ALU = mybir.AluOpType
ACT = mybir.ActivationFunctionType

P = 128
NT = B // P
GT = 4
NG = NT // GT
ON_SCALAR = [3]
BANK_DT = F32


def tile_emaaggregator_pa_t_kernel(tc, z, W1, b1, g1, be1, W2, b2, g2, be2, out):
    nc = tc.nc
    z_view = z.rearrange("(p i) k -> p i k", i=NT)
    out_view = out.rearrange("(p i) d -> p i d", i=NT)

    with ExitStack() as ctx:
        const = ctx.enter_context(tc.tile_pool(name="const", bufs=1))
        work = ctx.enter_context(tc.tile_pool(name="work", bufs=2))
        stats = ctx.enter_context(tc.tile_pool(name="stats", bufs=3))
        psum = ctx.enter_context(tc.psum_pool(name="psum", bufs=2))
        ctx.enter_context(tc.manual_schedule())

        live = {}

        def ok(grp):
            return 0 <= grp < NG

        b1n = const.tile([P, F], BF16, name="b1n")
        nc.scalar.dma_start(out=b1n[:], in_=b1.partition_broadcast(P))

        zs = []
        w1raw = []
        w2raw = []

        def load_z(grp):
            t = const.tile([P, GT, D], BF16, name="zs%d" % grp)
            nc.sync.dma_start(out=t[:], in_=z_view[:, GT * grp : GT * (grp + 1), :])
            zs.append(t)

        load_z(0)
        w1_view = W1.rearrange("(p j) c -> p j c", j=4)
        for g in range(2):
            t = const.tile([P, 4, 512], BF16, name="w1raw%d" % g)
            nc.sync.dma_start(out=t[:], in_=w1_view[:, :, 512 * g : 512 * (g + 1)])
            w1raw.append(t)
        load_z(1)
        for g in range(2):
            t = const.tile([P, 4, 512], BF16, name="w2raw%d" % g)
            nc.sync.dma_start(out=t[:], in_=W2[512 * g : 512 * (g + 1), :].rearrange("(p j) d -> p j d", j=4))
            w2raw.append(t)
        for grp in range(2, NG):
            load_z(grp)
        g1b = const.tile([P, 2, 4], BF16, name="g1b")
        nc.sync.dma_start(out=g1b[:], in_=g1.rearrange("(g p t) -> p g t", g=2, t=4))
        be1b = const.tile([P, 2, 4], BF16, name="be1b")
        nc.sync.dma_start(out=be1b[:], in_=be1.rearrange("(g p t) -> p g t", g=2, t=4))
        b2bc = const.tile([P, D], BF16, name="b2bc")
        nc.sync.dma_start(out=b2bc[:], in_=b2.partition_broadcast(P))
        g2bc = const.tile([P, D], BF16, name="g2bc")
        nc.sync.dma_start(out=g2bc[:], in_=g2.partition_broadcast(P))
        be2bc = const.tile([P, D], BF16, name="be2bc")
        nc.sync.dma_start(out=be2bc[:], in_=be2.partition_broadcast(P))

        neg_half = const.tile([P, GT], F32, name="neg_half")
        nc.gpsimd.memset(neg_half[:], -0.5)
        warm = const.tile([P, 1], F32, name="warm")
        nc.scalar.activation(out=warm[:], in_=neg_half[:, 0:1], func=ACT.Gelu)
        ident = const.tile([P, P], F32, name="ident")
        make_identity(nc, ident[:])

        def z_transpose(grp, h):
            if not ok(grp):
                return
            zt = psum.tile([P, 2, 2, P], F32, name="zt", tag="bank", bufs=8)
            for jj in range(2):
                words = zs[grp][:, 2 * h + jj, :].bitcast(F32)
                for u in range(2):
                    nc.tensor.transpose(zt[:, jj, u, :], words[:, u:256:2], ident[:])
            live["zt", grp, h] = zt

        def z_copy(grp, h):
            if not ok(grp):
                return
            if h == 0:
                live["zg", grp] = work.tile([P, GT * P * 4], BF16, name="zg", tag="zg", bufs=2, align_bytes=64)
            zgw = live["zg", grp][:].bitcast(F32).rearrange("p (j r u) -> p j r u", j=GT, u=2)
            nc.scalar.copy(
                out=zgw[:, 2 * h : 2 * h + 2, :, :], in_=live["zt", grp, h][:].rearrange("p j u r -> p j r u")
            )

        def z_quantise(grp):
            if not ok(grp):
                return
            zc = work.tile([P, GT * P], U32, name="zc", tag="zc", bufs=2, align_bytes=64)
            zsc = work.tile([P, GT * P], U8, name="zsc", tag="zsc", bufs=2, align_bytes=64)
            nc.vector.quantize_mx(out=zc[:].bitcast(FP8X4), scales=zsc[:], in_=live["zg", grp][:])
            live["zq", grp] = (zc, zsc)

        def matmul_1(grp, i):
            if not ok(grp):
                return
            zc, zsc = live["zq", grp]
            cols = slice(P * i, P * (i + 1))
            for g in range(2):
                u = psum.tile([P, 512], BANK_DT, name="u", tag="bank", bufs=8)
                nc.tensor.matmul_mx(
                    out=u[:],
                    lhsT=zc[:, cols].bitcast(FP8X4),
                    lhsT_scale=zsc[:, cols],
                    rhs=w1c[g][:].bitcast(FP8X4),
                    rhs_scale=w1s[g][:],
                    start=True,
                    stop=True,
                )
                live["u", grp, i, g] = u

        def add_b1(grp, i):
            if not ok(grp):
                return
            x = work.tile([P, F], F32, name="x", tag="x", bufs=2)
            for g in range(2):
                half = slice(512 * g, 512 * (g + 1))
                nc.vector.tensor_tensor(out=x[:, half], in0=live["u", grp, i, g][:], in1=b1p[:, half], op=ALU.add)
            live["x", grp, i] = x

        def gelu(grp, i):
            if not ok(grp):
                return
            if i == 0:
                live["sa", grp] = stats.tile([P, GT], F32, name="sa", tag="sa")
            a = work.tile([P, F], F32, name="a", tag="a", bufs=6)
            nc.scalar.activation(
                out=a[:], in_=live["x", grp, i][:], func=ACT.Gelu, accum_out=live["sa", grp][:, i : i + 1]
            )
            live["a", grp, i] = a

        def square_1(grp, i):
            if not ok(grp):
                return
            if i == 0:
                live["sq", grp] = stats.tile([P, GT], F32, name="sq", tag="sq")
            junk = work.tile([P, F], BF16, name="junk", tag="junk", bufs=1)
            nc.scalar.activation(
                out=junk[:],
                in_=live["a", grp, i][:],
                func=ACT.Square,
                scale=-float(F),
                bias=live["sa", grp][:, i : i + 1],
                accum_out=live["sq", grp][:, i : i + 1],
            )

        def neg_mean_1(grp):
            if not ok(grp):
                return
            nm = stats.tile([P, GT], F32, name="nm", tag="nm")
            nc.vector.tensor_scalar(out=nm[:], in0=live["sa", grp][:], scalar1=-1.0 / F, scalar2=None, op0=ALU.mult)
            live["nm", grp] = nm

        def var_eps_1(grp):
            if not ok(grp):
                return
            ve = stats.tile([P, GT], F32, name="ve", tag="ve")
            nc.vector.tensor_scalar(
                out=ve[:], in0=live["sq", grp][:], scalar1=1.0 / F**3, scalar2=EPS, op0=ALU.mult, op1=ALU.add
            )
            live["ve", grp] = ve

        def rstd_1(grp):
            if not ok(grp):
                return
            rs = stats.tile([P, GT], F32, name="rs", tag="rs")
            nc.gpsimd.tensor_tensor(out=rs[:], in0=live["ve", grp][:], in1=neg_half[:], op=ALU.pow)
            nr = stats.tile([P, GT], F32, name="nr", tag="nr")
            nc.gpsimd.tensor_tensor(out=nr[:], in0=live["nm", grp][:], in1=rs[:], op=ALU.mult)
            live["rs", grp] = rs
            live["nr", grp] = nr

        def normalise(grp, i):
            if not ok(grp):
                return
            col = slice(i, i + 1)
            xh = work.tile([P, F], F32, name="xh", tag="xh", bufs=4)
            if i in ON_SCALAR:
                nc.scalar.activation(
                    out=xh[:],
                    in_=live["a", grp, i][:],
                    func=ACT.Identity,
                    scale=live["rs", grp][:, col],
                    bias=live["nr", grp][:, col],
                )
            else:
                nc.vector.tensor_scalar(
                    out=xh[:],
                    in0=live["a", grp, i][:],
                    scalar1=live["nm", grp][:, col],
                    scalar2=live["rs", grp][:, col],
                    op0=ALU.add,
                    op1=ALU.mult,
                )
            live["xh", grp, i] = xh

        def h_transpose(grp, blk):
            if not ok(grp):
                return
            ht = psum.tile([P, GT * P], F32, name="ht", tag="bank", bufs=8)
            for i in range(GT):
                nc.tensor.transpose(ht[:, P * i : P * (i + 1)], live["xh", grp, i][:, P * blk : P * (blk + 1)], ident[:])
            live["ht", grp, blk] = ht

        def affine_1(grp, blk):
            if not ok(grp):
                return
            if blk == 0:
                live["hT", grp] = work.tile([P, 8, GT * P], BF16, name="hT", tag="hT", bufs=2)
            nc.scalar.activation(
                out=live["hT", grp][:, blk, :],
                in_=live["ht", grp, blk][:],
                func=ACT.Identity,
                scale=g1c[:, blk : blk + 1],
                bias=be1c[:, blk : blk + 1],
            )

        def interleave(grp, g):
            if not ok(grp):
                return
            hg = work.tile([P, GT * P, 4], BF16, name="hg", tag="hg", bufs=2, align_bytes=64)
            nc.vector.tensor_copy(
                out=hg[:].rearrange("p (c i) t -> p c t i", i=4),
                in_=live["hT", grp][:, 4 * g : 4 * g + 4, :].rearrange("p t (c i) -> p c t i", i=4),
            )
            live["hg", grp, g] = hg

        def h_quantise(grp, g):
            if not ok(grp):
                return
            hc = work.tile([P, GT * P], U32, name="hc", tag="hc", bufs=4, align_bytes=64)
            hs = work.tile([P, GT * P], U8, name="hs", tag="hs", bufs=4, align_bytes=64)
            nc.vector.quantize_mx(
                out=hc[:].bitcast(FP8X4), scales=hs[:], in_=live["hg", grp, g][:].rearrange("p n t -> p (n t)")
            )
            live["hq", grp, g] = (hc, hs)

        def matmul_2(grp, i):
            if not ok(grp):
                return
            cols = slice(P * i, P * (i + 1))
            o = psum.tile([P, D], F32, name="o", tag="bank", bufs=8)
            for g in range(2):
                hc, hs = live["hq", grp, g]
                nc.tensor.matmul_mx(
                    out=o[:],
                    lhsT=hc[:, cols].bitcast(FP8X4),
                    lhsT_scale=hs[:, cols],
                    rhs=w2c[g][:].bitcast(FP8X4),
                    rhs_scale=w2s[g][:],
                    start=(g == 0),
                    stop=(g == 1),
                )
            live["o", grp, i] = o

        def add_b2(grp, i):
            if not ok(grp):
                return
            if i == 0:
                live["sy", grp] = stats.tile([P, GT], F32, name="sy", tag="sy")
            y = work.tile([P, D], F32, name="y", tag="y", bufs=4)
            nc.vector.scalar_tensor_tensor(
                out=y[:],
                in0=live["o", grp, i][:],
                scalar=1.0,
                in1=b2bc[:],
                op0=ALU.mult,
                op1=ALU.add,
                accum_out=live["sy", grp][:, i : i + 1],
            )
            live["y", grp, i] = y

        def square_2(grp, i):
            if not ok(grp):
                return
            if i == 0:
                live["sq2", grp] = stats.tile([P, GT], F32, name="sq2", tag="sq2")
            junk2 = work.tile([P, D], BF16, name="junk2", tag="junk2", bufs=1)
            nc.scalar.activation(
                out=junk2[:],
                in_=live["y", grp, i][:],
                func=ACT.Square,
                scale=-float(D),
                bias=live["sy", grp][:, i : i + 1],
                accum_out=live["sq2", grp][:, i : i + 1],
            )

        def neg_mean_2(grp):
            if not ok(grp):
                return
            nm2 = stats.tile([P, GT], F32, name="nm2", tag="nm2")
            nc.vector.tensor_scalar(out=nm2[:], in0=live["sy", grp][:], scalar1=-1.0 / D, scalar2=None, op0=ALU.mult)
            live["nm2", grp] = nm2

        def var_eps_2(grp):
            if not ok(grp):
                return
            ve2 = stats.tile([P, GT], F32, name="ve2", tag="ve2")
            nc.vector.tensor_scalar(
                out=ve2[:], in0=live["sq2", grp][:], scalar1=1.0 / D**3, scalar2=EPS, op0=ALU.mult, op1=ALU.add
            )
            live["ve2", grp] = ve2

        def rstd_2(grp):
            if not ok(grp):
                return
            rs2 = stats.tile([P, GT], F32, name="rs2", tag="rs2")
            nc.gpsimd.tensor_tensor(out=rs2[:], in0=live["ve2", grp][:], in1=neg_half[:], op=ALU.pow)
            live["rs2", grp] = rs2

        def centre_gain(grp, i):
            if not ok(grp):
                return
            q = work.tile([P, D], F32, name="q", tag="q", bufs=4)
            nc.vector.scalar_tensor_tensor(
                out=q[:],
                in0=live["y", grp, i][:],
                scalar=live["nm2", grp][:, i : i + 1],
                in1=g2bc[:],
                op0=ALU.add,
                op1=ALU.mult,
            )
            live["q", grp, i] = q

        def scale_shift(grp, i):
            if not ok(grp):
                return
            ot = work.tile([P, D], F32, name="ot", tag="ot", bufs=4)
            nc.vector.scalar_tensor_tensor(
                out=ot[:],
                in0=live["q", grp, i][:],
                scalar=live["rs2", grp][:, i : i + 1],
                in1=be2bc[:],
                op0=ALU.mult,
                op1=ALU.add,
            )
            live["ot", grp, i] = ot

        def store(grp, i):
            if not ok(grp):
                return
            nc.sync.dma_start(out=out_view[:, GT * grp + i, :], in_=live["ot", grp, i][:])

        z_transpose(0, 0)
        w1g = []
        for g in range(2):
            w1g.append(const.tile([P, 2048], BF16, name="w1g%d" % g, align_bytes=64))
        dst = [w1g[g][:].rearrange("p (t m j) -> p t m j", t=4, j=4) for g in range(2)]
        src = [w1raw[g][:].rearrange("p j (m t) -> p t m j", t=4) for g in range(2)]
        w1c, w1s, w2c, w2s = [], [], [], []
        for g in range(2):
            w1c.append(const.tile([P, 512], U32, name="w1c%d" % g, align_bytes=64))
            w1s.append(const.tile([P, 512], U8, name="w1s%d" % g, align_bytes=64))
        nc.vector.tensor_copy(out=dst[0][:, 0:2], in_=src[0][:, 0:2])
        nc.vector.tensor_copy(out=dst[0][:, 2:4], in_=src[0][:, 2:4])
        nc.scalar.copy(out=dst[1][:, 2:4], in_=src[1][:, 2:4])
        z_copy(0, 0)
        z_transpose(0, 1)
        z_copy(0, 1)
        nc.vector.tensor_copy(out=dst[1][:, 0:2], in_=src[1][:, 0:2])
        nc.vector.quantize_mx(out=w1c[0][:].bitcast(FP8X4), scales=w1s[0][:], in_=w1g[0][:])
        z_quantise(0)
        nc.vector.quantize_mx(out=w1c[1][:].bitcast(FP8X4), scales=w1s[1][:], in_=w1g[1][:])
        b1p = const.tile([P, F], BF16, name="b1p")
        nc.scalar.copy(
            out=b1p[:].rearrange("p (g t m) -> p g t m", g=2, t=4),
            in_=b1n[:].rearrange("p (g m t) -> p g t m", g=2, t=4),
        )
        g1c = const.tile([P, 8], F32, name="g1c")
        nc.gpsimd.tensor_copy(out=g1c[:], in_=g1b[:].rearrange("p g t -> p (g t)"))
        be1c = const.tile([P, 8], F32, name="be1c")
        nc.gpsimd.tensor_copy(out=be1c[:], in_=be1b[:].rearrange("p g t -> p (g t)"))

        def prep_w2():
            w2g = []
            for g in range(2):
                w2g.append(const.tile([P, 512, 4], BF16, name="w2g%d" % g, align_bytes=64))
                nc.vector.tensor_copy(out=w2g[g][:], in_=w2raw[g][:].rearrange("p j d -> p d j"))
            for g in range(2):
                w2c.append(const.tile([P, 512], U32, name="w2c%d" % g, align_bytes=64))
                w2s.append(const.tile([P, 512], U8, name="w2s%d" % g, align_bytes=64))
                nc.vector.quantize_mx(
                    out=w2c[g][:].bitcast(FP8X4), scales=w2s[g][:], in_=w2g[g][:].rearrange("p d j -> p (d j)")
                )

        for step in range(NG + 2):
            if True:
                z_transpose(step + 1, 0)
                matmul_1(step, 0)
                matmul_1(step, 1)
                z_transpose(step + 1, 1)
                matmul_1(step, 2)
                var_eps_1(step - 1)
                neg_mean_1(step - 1)
                add_b1(step, 0)
                rstd_1(step - 1)
                normalise(step - 1, 0)
                normalise(step - 1, 1)
                z_copy(step + 1, 0)
                normalise(step - 1, 2)
                normalise(step - 1, 3)
                h_transpose(step - 1, 0)
                centre_gain(step - 2, 0)
                gelu(step, 0)
                var_eps_2(step - 2)
                centre_gain(step - 2, 1)
                h_transpose(step - 1, 1)
                rstd_2(step - 2)
                add_b1(step, 1)
                h_transpose(step - 1, 2)
                z_copy(step + 1, 1)
                h_transpose(step - 1, 3)
                affine_1(step - 1, 0)
                add_b1(step, 2)
                h_transpose(step - 1, 4)
                affine_1(step - 1, 1)
                h_transpose(step - 1, 5)
                h_transpose(step - 1, 6)
                affine_1(step - 1, 2)
                z_quantise(step + 1)
                h_transpose(step - 1, 7)
                affine_1(step - 1, 3)
                centre_gain(step - 2, 2)
                matmul_1(step, 3)
                affine_1(step - 1, 4)
                interleave(step - 1, 0)
                affine_1(step - 1, 5)
                affine_1(step - 1, 6)
                centre_gain(step - 2, 3)
                affine_1(step - 1, 7)
                h_quantise(step - 1, 0)
                gelu(step, 1)
                interleave(step - 1, 1)
                square_1(step, 0)
                h_quantise(step - 1, 1)
                matmul_2(step - 1, 0)
                square_1(step, 1)
                add_b1(step, 3)
                matmul_2(step - 1, 1)
                gelu(step, 2)
                scale_shift(step - 2, 0)
                matmul_2(step - 1, 2)
                scale_shift(step - 2, 1)
                store(step - 2, 0)
                matmul_2(step - 1, 3)
                square_1(step, 2)
                scale_shift(step - 2, 2)
                store(step - 2, 1)
                add_b2(step - 1, 0)
                store(step - 2, 2)
                gelu(step, 3)
                add_b2(step - 1, 1)
                add_b2(step - 1, 2)
                square_1(step, 3)
                add_b2(step - 1, 3)
                scale_shift(step - 2, 3)
                square_2(step - 1, 0)
                neg_mean_2(step - 1)
                square_2(step - 1, 1)
                store(step - 2, 3)
                square_2(step - 1, 2)
                square_2(step - 1, 3)
            if step == 0:
                prep_w2()
